import numpy as np
import ml_dtypes

BF16 = ml_dtypes.bfloat16


def bf(x):
    return np.asarray(x, np.float32).astype(BF16)


def f32(x):
    return np.asarray(x, np.float32)


def f64(x):
    return np.asarray(x).astype(np.float64)


def striped(idx):
    return np.tile(idx.reshape(-1, 16).T, (8, 1))


S, D, N, STEPS = 256, 128, 1024, 3


def setup_inputs():
    return {"table": bf(np.random.standard_normal((S, D))), "w": bf(np.eye(D) + 0.03 * np.random.standard_normal((D, D))), "b": f32(0.1 * np.random.standard_normal((D, 1))), "offs": striped(np.concatenate([np.random.permutation(S) for _ in range(-(-(N) // S))])[:N])}


def reference(table, w, b, offs):
    idx = offs[:16].T.reshape(-1)
    h = f64(table)[idx].T
    for _ in range(STEPS):
        h = f64(w).T @ h + f64(b)
    return h

@@ -1,0 +1,66 @@
+import concourse.mybir as mybir
+from concourse.masks import make_identity
+
+BF16, F32, U16 = mybir.dt.bfloat16, mybir.dt.float32, mybir.dt.uint16
+IDENTITY = mybir.ActivationFunctionType.Identity
+
+P = 128
+S = 256
+N = 1024
+STEPS = 3
+PIECE = 256
+PIECES = N // PIECE
+
+FLOPS = 2 * STEPS * P * P * N
+
+
+def tile_tmpnn_kernel(tc, table, w, b, offs, out):
+    nc = tc.nc
+    with (
+        tc.tile_pool(name="held", bufs=1) as held,
+        tc.tile_pool(name="hidden", bufs=(STEPS - 1) * PIECES) as hidden,
+        tc.tile_pool(name="results", bufs=PIECES) as results,
+        tc.psum_pool(name="flip", bufs=1) as flip,
+        tc.psum_pool(name="products", bufs=6) as products,
+    ):
+        offsets = held.tile([P, N // 16], U16, name="offsets")
+        nc.sync.dma_start(offsets[:], offs)
+
+        rows = held.tile([P, S // P, P], BF16, name="rows")
+        nc.scalar.dma_start(rows[:], table.rearrange("(t p) k -> p t k", p=P))
+        weights = held.tile([P, P], BF16, name="weights")
+        nc.sync.dma_start(weights[:], w)
+        bias = held.tile([P, 1], F32, name="bias")
+        nc.sync.dma_start(bias[:], b)
+
+        identity = held.tile([P, P], BF16, name="identity")
+        make_identity(nc, identity[:])
+        flipped = flip.tile([P, S], BF16, name="flipped")
+        for t in range(S // P):
+            nc.tensor.transpose(flipped[:, t * P : (t + 1) * P], rows[:, t, :], identity[:])
+        window = held.tile([P, S], BF16, name="window")
+        nc.vector.tensor_copy(window[:], flipped[:])
+
+        def add_bias(piece, target, product):
+            if piece % 2 == 0:
+                nc.vector.tensor_scalar_add(target, product, bias[:])
+            else:
+                nc.scalar.activation(target, product, IDENTITY, bias=bias[:])
+
+        columns = PIECE // 16
+        moving = [
+            window[:].indirect(offsets[:, piece * columns : (piece + 1) * columns])
+            for piece in range(PIECES)
+        ]
+        for step in range(STEPS):
+            for piece in range(PIECES):
+                product = products.tile([P, PIECE], F32, name="product")
+                nc.tensor.matmul(product[:], weights[:], moving[piece])
+                if step < STEPS - 1:
+                    h = hidden.tile([P, PIECE], BF16, name="h")
+                    add_bias(piece, h[:], product[:])
+                    moving[piece] = h[:]
+                else:
+                    result = results.tile([P, PIECE], F32, name="result")
+                    add_bias(piece, result[:], product[:])
+                    nc.sync.dma_start(out[:, piece * PIECE : (piece + 1) * PIECE], result[:])

@@ -33,6 +33,10 @@ def tile_tmpnn_kernel(tc, table, w, b, offs, out):
         bias = held.tile([P, 1], F32, name="bias")
         nc.sync.dma_start(bias[:], b)
 
+        scratch = held.tile([P, 1], F32, name="scratch")
+        nc.vector.memset(scratch[:], 0.0)
+        nc.scalar.activation(scratch[:], scratch[:], IDENTITY)
+
         identity = held.tile([P, P], BF16, name="identity")
         make_identity(nc, identity[:])
         flipped = flip.tile([P, S], BF16, name="flipped")

@@ -10,6 +10,8 @@ N = 1024
 STEPS = 3
 PIECE = 256
 PIECES = N // PIECE
+BANK = 512
+WARM_UPS = 4
 
 FLOPS = 2 * STEPS * P * P * N
 
@@ -36,6 +38,12 @@ def tile_tmpnn_kernel(tc, table, w, b, offs, out):
         scratch = held.tile([P, 1], F32, name="scratch")
         nc.vector.memset(scratch[:], 0.0)
         nc.scalar.activation(scratch[:], scratch[:], IDENTITY)
+
+        zeros = held.tile([P, BANK], BF16, name="zeros")
+        nc.vector.memset(zeros[:], 0.0)
+        unread = flip.tile([P, BANK], F32, name="unread")
+        for turn in range(WARM_UPS):
+            nc.tensor.matmul(unread[:], zeros[:, :P], zeros[:])
 
         identity = held.tile([P, P], BF16, name="identity")
         make_identity(nc, identity[:])

@@ -11,7 +11,7 @@ STEPS = 3
 PIECE = 256
 PIECES = N // PIECE
 BANK = 512
-WARM_UPS = 4
+WARM_UPS = 6
 
 FLOPS = 2 * STEPS * P * P * N
 

@@ -10,8 +10,7 @@ N = 1024
 STEPS = 3
 PIECE = 256
 PIECES = N // PIECE
-BANK = 512
-WARM_UPS = 6
+WARM_UPS = 12
 
 FLOPS = 2 * STEPS * P * P * N
 
@@ -35,15 +34,15 @@ def tile_tmpnn_kernel(tc, table, w, b, offs, out):
         bias = held.tile([P, 1], F32, name="bias")
         nc.sync.dma_start(bias[:], b)
 
+        zeros = held.tile([P, P], BF16, name="zeros")
+        nc.vector.memset(zeros[:], 0.0)
+        unread = flip.tile([P, P], F32, name="unread")
+        for turn in range(WARM_UPS):
+            nc.tensor.matmul(unread[:], zeros[:], zeros[:])
+
         scratch = held.tile([P, 1], F32, name="scratch")
         nc.vector.memset(scratch[:], 0.0)
         nc.scalar.activation(scratch[:], scratch[:], IDENTITY)
-
-        zeros = held.tile([P, BANK], BF16, name="zeros")
-        nc.vector.memset(zeros[:], 0.0)
-        unread = flip.tile([P, BANK], F32, name="unread")
-        for turn in range(WARM_UPS):
-            nc.tensor.matmul(unread[:], zeros[:, :P], zeros[:])
 
         identity = held.tile([P, P], BF16, name="identity")
         make_identity(nc, identity[:])

@@ -24,11 +24,11 @@ def tile_tmpnn_kernel(tc, table, w, b, offs, out):
         tc.psum_pool(name="flip", bufs=1) as flip,
         tc.psum_pool(name="products", bufs=6) as products,
     ):
+        rows = held.tile([P, S // P, P], BF16, name="rows")
+        nc.sync.dma_start(rows[:], table.rearrange("(t p) k -> p t k", p=P))
+
         offsets = held.tile([P, N // 16], U16, name="offsets")
         nc.sync.dma_start(offsets[:], offs)
-
-        rows = held.tile([P, S // P, P], BF16, name="rows")
-        nc.scalar.dma_start(rows[:], table.rearrange("(t p) k -> p t k", p=P))
         weights = held.tile([P, P], BF16, name="weights")
         nc.sync.dma_start(weights[:], w)
         bias = held.tile([P, 1], F32, name="bias")

@@ -45,7 +45,8 @@ def tile_tmpnn_kernel(tc, table, w, b, offs, out):
         nc.scalar.activation(scratch[:], scratch[:], IDENTITY)
 
         identity = held.tile([P, P], BF16, name="identity")
-        make_identity(nc, identity[:])
+        nc.vector.memset(identity[:], 0.0)
+        make_identity(nc, identity[:], nomemset=True)
         flipped = flip.tile([P, S], BF16, name="flipped")
         for t in range(S // P):
             nc.tensor.transpose(flipped[:, t * P : (t + 1) * P], rows[:, t, :], identity[:])

@@ -8,8 +8,7 @@ P = 128
 S = 256
 N = 1024
 STEPS = 3
-PIECE = 256
-PIECES = N // PIECE
+WIDTHS = (192, 192, 128)
 WARM_UPS = 12
 
 FLOPS = 2 * STEPS * P * P * N
@@ -19,8 +18,8 @@ def tile_tmpnn_kernel(tc, table, w, b, offs, out):
     nc = tc.nc
     with (
         tc.tile_pool(name="held", bufs=1) as held,
-        tc.tile_pool(name="hidden", bufs=(STEPS - 1) * PIECES) as hidden,
-        tc.tile_pool(name="results", bufs=PIECES) as results,
+        tc.tile_pool(name="hidden", bufs=2 * (STEPS - 1) * len(WIDTHS)) as hidden,
+        tc.tile_pool(name="results", bufs=len(WIDTHS)) as results,
         tc.psum_pool(name="flip", bufs=1) as flip,
         tc.psum_pool(name="products", bufs=6) as products,
     ):
@@ -53,26 +52,31 @@ def tile_tmpnn_kernel(tc, table, w, b, offs, out):
         window = held.tile([P, S], BF16, name="window")
         nc.vector.tensor_copy(window[:], flipped[:])
 
-        def add_bias(piece, target, product):
-            if piece % 2 == 0:
+        def add_bias(half, target, product):
+            if half == 0:
                 nc.vector.tensor_scalar_add(target, product, bias[:])
             else:
                 nc.scalar.activation(target, product, IDENTITY, bias=bias[:])
 
-        columns = PIECE // 16
-        moving = [
-            window[:].indirect(offsets[:, piece * columns : (piece + 1) * columns])
-            for piece in range(PIECES)
-        ]
+        starts = [2 * sum(WIDTHS[:pair]) for pair in range(len(WIDTHS))]
+        moving = {}
+        for pair, width in enumerate(WIDTHS):
+            for half in range(2):
+                first = (starts[pair] + half * width) // 16
+                moving[pair, half] = window[:].indirect(offsets[:, first : first + width // 16])
+
         for step in range(STEPS):
-            for piece in range(PIECES):
-                product = products.tile([P, PIECE], F32, name="product")
-                nc.tensor.matmul(product[:], weights[:], moving[piece])
-                if step < STEPS - 1:
-                    h = hidden.tile([P, PIECE], BF16, name="h")
-                    add_bias(piece, h[:], product[:])
-                    moving[piece] = h[:]
-                else:
-                    result = results.tile([P, PIECE], F32, name="result")
-                    add_bias(piece, result[:], product[:])
-                    nc.sync.dma_start(out[:, piece * PIECE : (piece + 1) * PIECE], result[:])
+            for pair, width in enumerate(WIDTHS):
+                if step == STEPS - 1:
+                    result = results.tile([P, 2 * width], F32, name="result")
+                for half in range(2):
+                    product = products.tile([P, width], F32, name="product")
+                    nc.tensor.matmul(product[:], weights[:], moving[pair, half])
+                    if step < STEPS - 1:
+                        h = hidden.tile([P, width], BF16, name="h")
+                        add_bias(half, h[:], product[:])
+                        moving[pair, half] = h[:]
+                    else:
+                        add_bias(half, result[:, half * width : (half + 1) * width], product[:])
+                if step == STEPS - 1:
+                    nc.sync.dma_start(out[:, starts[pair] : starts[pair] + 2 * width], result[:])

@@ -8,7 +8,7 @@ P = 128
 S = 256
 N = 1024
 STEPS = 3
-WIDTHS = (192, 192, 128)
+WIDTHS = (128, 128, 128, 128)
 WARM_UPS = 12
 
 FLOPS = 2 * STEPS * P * P * N
@@ -21,7 +21,7 @@ def tile_tmpnn_kernel(tc, table, w, b, offs, out):
         tc.tile_pool(name="hidden", bufs=2 * (STEPS - 1) * len(WIDTHS)) as hidden,
         tc.tile_pool(name="results", bufs=len(WIDTHS)) as results,
         tc.psum_pool(name="flip", bufs=1) as flip,
-        tc.psum_pool(name="products", bufs=6) as products,
+        tc.psum_pool(name="products", bufs=7) as products,
     ):
         rows = held.tile([P, S // P, P], BF16, name="rows")
         nc.sync.dma_start(rows[:], table.rearrange("(t p) k -> p t k", p=P))
@@ -35,7 +35,7 @@ def tile_tmpnn_kernel(tc, table, w, b, offs, out):
 
         zeros = held.tile([P, P], BF16, name="zeros")
         nc.vector.memset(zeros[:], 0.0)
-        unread = flip.tile([P, P], F32, name="unread")
+        unread = flip.tile([P, P], F32, name="unread", tag="flip")
         for turn in range(WARM_UPS):
             nc.tensor.matmul(unread[:], zeros[:], zeros[:])
 
@@ -46,7 +46,7 @@ def tile_tmpnn_kernel(tc, table, w, b, offs, out):
         identity = held.tile([P, P], BF16, name="identity")
         nc.vector.memset(identity[:], 0.0)
         make_identity(nc, identity[:], nomemset=True)
-        flipped = flip.tile([P, S], BF16, name="flipped")
+        flipped = flip.tile([P, S], BF16, name="flipped", tag="flip")
         for t in range(S // P):
             nc.tensor.transpose(flipped[:, t * P : (t + 1) * P], rows[:, t, :], identity[:])
         window = held.tile([P, S], BF16, name="window")

@@ -35,7 +35,7 @@ def tile_tmpnn_kernel(tc, table, w, b, offs, out):
 
         zeros = held.tile([P, P], BF16, name="zeros")
         nc.vector.memset(zeros[:], 0.0)
-        unread = flip.tile([P, P], F32, name="unread", tag="flip")
+        unread = products.tile([P, P], F32, name="unread", tag="product")
         for turn in range(WARM_UPS):
             nc.tensor.matmul(unread[:], zeros[:], zeros[:])
 
@@ -46,7 +46,7 @@ def tile_tmpnn_kernel(tc, table, w, b, offs, out):
         identity = held.tile([P, P], BF16, name="identity")
         nc.vector.memset(identity[:], 0.0)
         make_identity(nc, identity[:], nomemset=True)
-        flipped = flip.tile([P, S], BF16, name="flipped", tag="flip")
+        flipped = flip.tile([P, S], BF16, name="flipped")
         for t in range(S // P):
             nc.tensor.transpose(flipped[:, t * P : (t + 1) * P], rows[:, t, :], identity[:])
         window = held.tile([P, S], BF16, name="window")

@@ -20,11 +20,14 @@ def tile_tmpnn_kernel(tc, table, w, b, offs, out):
         tc.tile_pool(name="held", bufs=1) as held,
         tc.tile_pool(name="hidden", bufs=2 * (STEPS - 1) * len(WIDTHS)) as hidden,
         tc.tile_pool(name="results", bufs=len(WIDTHS)) as results,
-        tc.psum_pool(name="flip", bufs=1) as flip,
-        tc.psum_pool(name="products", bufs=7) as products,
+        tc.psum_pool(name="flip", bufs=S // P) as flip,
+        tc.psum_pool(name="products", bufs=6) as products,
     ):
-        rows = held.tile([P, S // P, P], BF16, name="rows")
-        nc.sync.dma_start(rows[:], table.rearrange("(t p) k -> p t k", p=P))
+        rows = []
+        for t in range(S // P):
+            half_of_store = held.tile([P, P], BF16, name="rows%d" % t)
+            nc.sync.dma_start(half_of_store[:], table[t * P : (t + 1) * P, :])
+            rows.append(half_of_store)
 
         offsets = held.tile([P, N // 16], U16, name="offsets")
         nc.sync.dma_start(offsets[:], offs)
@@ -46,11 +49,11 @@ def tile_tmpnn_kernel(tc, table, w, b, offs, out):
         identity = held.tile([P, P], BF16, name="identity")
         nc.vector.memset(identity[:], 0.0)
         make_identity(nc, identity[:], nomemset=True)
-        flipped = flip.tile([P, S], BF16, name="flipped")
-        for t in range(S // P):
-            nc.tensor.transpose(flipped[:, t * P : (t + 1) * P], rows[:, t, :], identity[:])
         window = held.tile([P, S], BF16, name="window")
-        nc.vector.tensor_copy(window[:], flipped[:])
+        for t in range(S // P):
+            flipped = flip.tile([P, P], BF16, name="flipped")
+            nc.tensor.transpose(flipped[:], rows[t][:], identity[:])
+            nc.vector.tensor_copy(window[:, t * P : (t + 1) * P], flipped[:])
 
         def add_bias(half, target, product):
             if half == 0:

@@ -8,7 +8,7 @@ P = 128
 S = 256
 N = 1024
 STEPS = 3
-WIDTHS = (128, 128, 128, 128)
+WIDTHS = (192, 192, 128)
 WARM_UPS = 12
 
 FLOPS = 2 * STEPS * P * P * N

@@ -8,7 +8,9 @@ P = 128
 S = 256
 N = 1024
 STEPS = 3
-WIDTHS = (192, 192, 128)
+PIECE = 128
+PAIRS = N // (2 * PIECE)
+STORES = (1, 2, 1)
 WARM_UPS = 12
 
 FLOPS = 2 * STEPS * P * P * N
@@ -18,10 +20,9 @@ def tile_tmpnn_kernel(tc, table, w, b, offs, out):
     nc = tc.nc
     with (
         tc.tile_pool(name="held", bufs=1) as held,
-        tc.tile_pool(name="hidden", bufs=2 * (STEPS - 1) * len(WIDTHS)) as hidden,
-        tc.tile_pool(name="results", bufs=len(WIDTHS)) as results,
-        tc.psum_pool(name="flip", bufs=S // P) as flip,
-        tc.psum_pool(name="products", bufs=6) as products,
+        tc.tile_pool(name="hidden", bufs=2 * (STEPS - 1) * PAIRS) as hidden,
+        tc.tile_pool(name="results", bufs=1) as results,
+        tc.psum_pool(name="banks", bufs=8) as banks,
     ):
         rows = []
         for t in range(S // P):
@@ -38,7 +39,7 @@ def tile_tmpnn_kernel(tc, table, w, b, offs, out):
 
         zeros = held.tile([P, P], BF16, name="zeros")
         nc.vector.memset(zeros[:], 0.0)
-        unread = products.tile([P, P], F32, name="unread", tag="product")
+        unread = banks.tile([P, P], F32, name="unread", tag="bank")
         for turn in range(WARM_UPS):
             nc.tensor.matmul(unread[:], zeros[:], zeros[:])
 
@@ -51,7 +52,7 @@ def tile_tmpnn_kernel(tc, table, w, b, offs, out):
         make_identity(nc, identity[:], nomemset=True)
         window = held.tile([P, S], BF16, name="window")
         for t in range(S // P):
-            flipped = flip.tile([P, P], BF16, name="flipped")
+            flipped = banks.tile([P, P], BF16, name="flipped", tag="bank")
             nc.tensor.transpose(flipped[:], rows[t][:], identity[:])
             nc.vector.tensor_copy(window[:, t * P : (t + 1) * P], flipped[:])
 
@@ -61,25 +62,29 @@ def tile_tmpnn_kernel(tc, table, w, b, offs, out):
             else:
                 nc.scalar.activation(target, product, IDENTITY, bias=bias[:])
 
-        starts = [2 * sum(WIDTHS[:pair]) for pair in range(len(WIDTHS))]
-        moving = {}
-        for pair, width in enumerate(WIDTHS):
-            for half in range(2):
-                first = (starts[pair] + half * width) // 16
-                moving[pair, half] = window[:].indirect(offsets[:, first : first + width // 16])
+        columns = PIECE // 16
+        moving = [
+            window[:].indirect(offsets[:, piece * columns : (piece + 1) * columns])
+            for piece in range(2 * PAIRS)
+        ]
 
-        for step in range(STEPS):
-            for pair, width in enumerate(WIDTHS):
-                if step == STEPS - 1:
-                    result = results.tile([P, 2 * width], F32, name="result")
-                for half in range(2):
-                    product = products.tile([P, width], F32, name="product")
-                    nc.tensor.matmul(product[:], weights[:], moving[pair, half])
-                    if step < STEPS - 1:
-                        h = hidden.tile([P, width], BF16, name="h")
-                        add_bias(half, h[:], product[:])
-                        moving[pair, half] = h[:]
-                    else:
-                        add_bias(half, result[:, half * width : (half + 1) * width], product[:])
-                if step == STEPS - 1:
-                    nc.sync.dma_start(out[:, starts[pair] : starts[pair] + 2 * width], result[:])
+        def step_of(piece, target):
+            product = banks.tile([P, PIECE], F32, name="product", tag="bank")
+            nc.tensor.matmul(product[:], weights[:], moving[piece])
+            add_bias(piece % 2, target, product[:])
+
+        for step in range(STEPS - 1):
+            for piece in range(2 * PAIRS):
+                h = hidden.tile([P, PIECE], BF16, name="h")
+                step_of(piece, h[:])
+                moving[piece] = h[:]
+
+        piece = 0
+        for store, pairs in enumerate(STORES):
+            first = piece * PIECE
+            width = 2 * pairs * PIECE
+            result = results.tile([P, width], F32, name="result%d" % store)
+            for place in range(0, width, PIECE):
+                step_of(piece, result[:, place : place + PIECE])
+                piece += 1
+            nc.sync.dma_start(out[:, first : first + width], result[:])

@@ -11,7 +11,7 @@ STEPS = 3
 PIECE = 128
 PAIRS = N // (2 * PIECE)
 STORES = (1, 2, 1)
-WARM_UPS = 12
+WARM_UPS = 11
 
 FLOPS = 2 * STEPS * P * P * N
 
@@ -27,7 +27,8 @@ def tile_tmpnn_kernel(tc, table, w, b, offs, out):
         rows = []
         for t in range(S // P):
             half_of_store = held.tile([P, P], BF16, name="rows%d" % t)
-            nc.sync.dma_start(half_of_store[:], table[t * P : (t + 1) * P, :])
+            queue = nc.sync if t == 0 else nc.scalar
+            queue.dma_start(half_of_store[:], table[t * P : (t + 1) * P, :])
             rows.append(half_of_store)
 
         offsets = held.tile([P, N // 16], U16, name="offsets")

import concourse.mybir as mybir
from concourse.masks import make_identity

BF16, F32, U16 = mybir.dt.bfloat16, mybir.dt.float32, mybir.dt.uint16
IDENTITY = mybir.ActivationFunctionType.Identity

P = 128
S = 256
N = 1024
STEPS = 3
PIECE = 128
PAIRS = N // (2 * PIECE)
STORES = (1, 2, 1)
WARM_UPS = 11

FLOPS = 2 * STEPS * P * P * N


def tile_tmpnn_kernel(tc, table, w, b, offs, out):
    nc = tc.nc
    with (
        tc.tile_pool(name="held", bufs=1) as held,
        tc.tile_pool(name="hidden", bufs=2 * (STEPS - 1) * PAIRS) as hidden,
        tc.tile_pool(name="results", bufs=1) as results,
        tc.psum_pool(name="banks", bufs=8) as banks,
    ):
        rows = []
        for t in range(S // P):
            half_of_store = held.tile([P, P], BF16, name="rows%d" % t)
            queue = nc.sync if t == 0 else nc.scalar
            queue.dma_start(half_of_store[:], table[t * P : (t + 1) * P, :])
            rows.append(half_of_store)

        offsets = held.tile([P, N // 16], U16, name="offsets")
        nc.sync.dma_start(offsets[:], offs)
        weights = held.tile([P, P], BF16, name="weights")
        nc.sync.dma_start(weights[:], w)
        bias = held.tile([P, 1], F32, name="bias")
        nc.sync.dma_start(bias[:], b)

        zeros = held.tile([P, P], BF16, name="zeros")
        nc.vector.memset(zeros[:], 0.0)
        unread = banks.tile([P, P], F32, name="unread", tag="bank")
        for turn in range(WARM_UPS):
            nc.tensor.matmul(unread[:], zeros[:], zeros[:])

        scratch = held.tile([P, 1], F32, name="scratch")
        nc.vector.memset(scratch[:], 0.0)
        nc.scalar.activation(scratch[:], scratch[:], IDENTITY)

        identity = held.tile([P, P], BF16, name="identity")
        nc.vector.memset(identity[:], 0.0)
        make_identity(nc, identity[:], nomemset=True)
        window = held.tile([P, S], BF16, name="window")
        for t in range(S // P):
            flipped = banks.tile([P, P], BF16, name="flipped", tag="bank")
            nc.tensor.transpose(flipped[:], rows[t][:], identity[:])
            nc.vector.tensor_copy(window[:, t * P : (t + 1) * P], flipped[:])

        def add_bias(half, target, product):
            if half == 0:
                nc.vector.tensor_scalar_add(target, product, bias[:])
            else:
                nc.scalar.activation(target, product, IDENTITY, bias=bias[:])

        columns = PIECE // 16
        moving = [
            window[:].indirect(offsets[:, piece * columns : (piece + 1) * columns])
            for piece in range(2 * PAIRS)
        ]

        def step_of(piece, target):
            product = banks.tile([P, PIECE], F32, name="product", tag="bank")
            nc.tensor.matmul(product[:], weights[:], moving[piece])
            add_bias(piece % 2, target, product[:])

        for step in range(STEPS - 1):
            for piece in range(2 * PAIRS):
                h = hidden.tile([P, PIECE], BF16, name="h")
                step_of(piece, h[:])
                moving[piece] = h[:]

        piece = 0
        for store, pairs in enumerate(STORES):
            first = piece * PIECE
            width = 2 * pairs * PIECE
            result = results.tile([P, width], F32, name="result%d" % store)
            for place in range(0, width, PIECE):
                step_of(piece, result[:, place : place + PIECE])
                piece += 1
            nc.sync.dma_start(out[:, first : first + width], result[:])
